import numpy as np
import ml_dtypes


def mxq(x, axis, fmt="e4m3"):
    dtype, down = {"e4m3": (ml_dtypes.float8_e4m3fn, 7), "e5m2": (ml_dtypes.float8_e5m2, 14)}[fmt]
    v = np.moveaxis(np.asarray(x, np.float32).astype(ml_dtypes.bfloat16).astype(np.float64), axis, -1)
    blocks = v.reshape(v.shape[:-1] + (-1, 32))
    amax = np.abs(blocks).max(-1, keepdims=True)
    byte = np.maximum(np.where(amax > 0, np.frexp(amax)[1] - 1 + 127, 0) - down, 1)
    scale = np.exp2(byte - 127.0)
    codes = (blocks / scale).astype(np.float32).astype(dtype).astype(np.float64)
    return np.moveaxis((codes * scale).reshape(v.shape), -1, axis)


WIDE = False


def mx_kscale(k):
    if not WIDE:
        return np.ones(k)
    levels = np.array([10, -10, 5, -5, 0])
    if k % 512:
        return np.exp2(np.random.permutation(np.resize(levels, k // 32))).repeat(32)
    a = np.empty((k // 512, 16))
    for p in range(k // 512):
        a[p, :8] = np.random.permutation(np.resize(levels, 8))
        for g in range(8):
            far = levels[np.abs(levels - a[p, g]) >= 10]
            a[p, g + 8] = far[np.random.randint(len(far))]
    return np.exp2(a.ravel()).repeat(32)


BF16 = ml_dtypes.bfloat16


def bf(x):
    return np.asarray(x, np.float32).astype(BF16)


def f64(x):
    return np.asarray(x).astype(np.float64)


B, S, D, F, N = 8, 1024, 512, 512, 256
SPARSITY = 0.1


def make_theta_sign(d1, d2, gain, row, col):
    mask = np.random.random((d1, d2)) < SPARSITY
    mag = np.abs(np.random.standard_normal((d1, d2))) * gain / np.sqrt(SPARSITY * d1)
    th = np.where(mask, mag, -mag) / row[:, None] * col
    sign = np.where(np.random.random((d1, d2)) < 0.5, -1.0, 1.0)
    return bf(th), bf(sign)


def setup_inputs():
    s, t = mx_kscale(D), mx_kscale(F)
    x = bf(np.random.standard_normal((B, S, D)) * s)
    th1, sign1 = make_theta_sign(D, F, 1.0, s, t)
    th2, sign2 = make_theta_sign(F, N, 1.4, t, np.ones(N))
    return {"x": x, "th1": th1, "sign1": sign1, "th2": th2, "sign2": sign2, "relu": 1}


def reference(x, th1, sign1, th2, sign2, relu):
    x = f64(x)
    for th, sign in ((f64(th1), f64(sign1)), (f64(th2), f64(sign2))):
        w = th * sign * (th > 0)
        x = mxq(x, 2, "e4m3") @ mxq(w, 0, "e4m3")
        if relu:
            x = np.maximum(x, 0.0)
    return x

@@ -1,0 +1,275 @@
+from contextlib import ExitStack
+
+import concourse.masks as masks
+import concourse.mybir as mybir
+
+F32 = mybir.dt.float32
+BF16 = mybir.dt.bfloat16
+U32 = mybir.dt.uint32
+U8 = mybir.dt.uint8
+FP8X4 = mybir.dt.float8_e4m3fn_x4
+ALU = mybir.AluOpType
+ACT = mybir.ActivationFunctionType
+
+P = 128
+PACK = 4
+TOKENS = 8192
+D = 512
+F = 512
+N = 256
+BANK = 512
+TILES = TOKENS // P
+ROUND = 4
+ROUNDS = TILES // ROUND
+AHEAD = 3
+BEHIND = 2
+
+FLOPS = 2 * TOKENS * D * (F + N)
+
+
+def x_copy_engine(r):
+    return "scalar" if r < AHEAD else "vector"
+
+
+def h_copy_engine(r, j):
+    return "vector" if (r, j) in ((ROUNDS - 2, 1), (ROUNDS - 2, 2), (ROUNDS - 1, 0), (ROUNDS - 1, 1)) else "scalar"
+
+
+def out_copy_engine(r, half):
+    if half == 0 or r in (4, ROUNDS - 4, ROUNDS - 3, ROUNDS - 2):
+        return "scalar"
+    return "vector"
+
+
+def x_quantise_parts(r):
+    return 2 if r == 0 else 1
+
+
+def h_quantise_parts(r):
+    return 2 if r >= ROUNDS - 2 else 1
+
+
+def store_parts(r):
+    return 2 if r >= ROUNDS - 3 else 1
+
+
+def tile_sparse_connect_t_kernel(tc, x, th1, sign1, th2, sign2, relu, out):
+    assert relu == 1
+    nc = tc.nc
+    x_rows = x.flatten_outer_dims().rearrange("(p j) k -> p (j k)", j=TILES)
+    out_rows = out.flatten_outer_dims().rearrange("(p j) n -> p (j n)", j=TILES)
+
+    with ExitStack() as ctx:
+        ctx.enter_context(tc.manual_schedule())
+        keep = ctx.enter_context(tc.tile_pool(name="keep", bufs=1))
+        ring = ctx.enter_context(tc.tile_pool(name="ring", bufs=4))
+        banks = ctx.enter_context(tc.psum_pool(name="banks", bufs=8))
+
+        th1_sb = keep.tile([P, PACK * F], BF16, name="th1_sb")
+        sign1_sb = keep.tile([P, PACK * F], BF16, name="sign1_sb")
+        th2_sb = keep.tile([P, PACK * N], BF16, name="th2_sb")
+        sign2_sb = keep.tile([P, PACK * N], BF16, name="sign2_sb")
+        x_sb = [keep.tile([P, ROUND * D], BF16, name="x_sb%d" % r) for r in range(ROUNDS)]
+        out_sb = [keep.tile([P, ROUND * N], F32, name="out_sb%d" % r) for r in range(ROUNDS)]
+
+        def load_w(dst, src):
+            nc.sync.dma_start(out=dst[:], in_=src.rearrange("(p t) n -> p (t n)", t=PACK))
+
+        def load_x(r):
+            nc.sync.dma_start(out=x_sb[r][:], in_=x_rows[:, r * ROUND * D : (r + 1) * ROUND * D])
+
+        load_w(th1_sb, th1)
+        load_w(sign1_sb, sign1)
+        for r in range(AHEAD):
+            load_x(r)
+        load_w(th2_sb, th2)
+        load_w(sign2_sb, sign2)
+        for r in range(AHEAD, ROUNDS):
+            load_x(r)
+
+        identity = keep.tile([P, P], F32, name="identity")
+        masks.make_identity(nc, identity[:])
+        warm_in = keep.tile([P, 1], F32, name="warm_in")
+        warm_out = keep.tile([P, 1], F32, name="warm_out")
+        nc.vector.memset(warm_in[:], 0.0)
+        nc.scalar.activation(out=warm_out[:], in_=warm_in[:], func=ACT.Relu)
+
+        w1_values = keep.tile([P, PACK * F], BF16, name="w1_values", align_bytes=64)
+        w1_words = keep.tile([P, F], U32, name="w1_words", align_bytes=64)
+        w1_scales = keep.tile([P, F], U8, name="w1_scales", align_bytes=64)
+        w2_values = keep.tile([P, PACK * N], BF16, name="w2_values", align_bytes=64)
+        w2_words = keep.tile([P, N], U32, name="w2_words", align_bytes=64)
+        w2_scales = keep.tile([P, N], U8, name="w2_scales", align_bytes=64)
+
+        def mask_w1_quarter(q):
+            nc.vector.scalar_tensor_tensor(
+                out=w1_values[:].rearrange("p (q m t) -> p q m t", q=4, m=P, t=PACK)[:, q],
+                in0=th1_sb[:].rearrange("p (t m q) -> p q m t", t=PACK, m=P, q=4)[:, q],
+                scalar=0.0,
+                in1=sign1_sb[:].rearrange("p (t m q) -> p q m t", t=PACK, m=P, q=4)[:, q],
+                op0=ALU.max,
+                op1=ALU.mult,
+            )
+
+        def quantise_w1():
+            nc.vector.quantize_mx(out=w1_words[:].bitcast(FP8X4), scales=w1_scales[:], in_=w1_values[:])
+
+        def mask_w2():
+            nc.vector.scalar_tensor_tensor(
+                out=w2_values[:].rearrange("p (n t) -> p n t", t=PACK),
+                in0=th2_sb[:].rearrange("p (t n) -> p n t", t=PACK),
+                scalar=0.0,
+                in1=sign2_sb[:].rearrange("p (t n) -> p n t", t=PACK),
+                op0=ALU.max,
+                op1=ALU.mult,
+            )
+
+        def quantise_w2():
+            nc.vector.quantize_mx(out=w2_words[:].bitcast(FP8X4), scales=w2_scales[:], in_=w2_values[:])
+
+        x_bank = {}
+        x_values = {}
+        x_words = {}
+        x_scales = {}
+        h_bank = {}
+        h_values = {}
+        h_words = {}
+        h_scales = {}
+        out_bank = {}
+
+        def relu_out_of_psum(engine, dst, src):
+            if engine == "scalar":
+                nc.scalar.activation(out=dst, in_=src, func=ACT.Relu)
+            else:
+                nc.vector.tensor_scalar_max(out=dst, in0=src, scalar1=0.0)
+
+        def quantise_part(words, scales, values, part, parts):
+            w = ROUND * P // parts
+            nc.vector.quantize_mx(
+                out=words[:, part * w : (part + 1) * w].bitcast(FP8X4),
+                scales=scales[:, part * w : (part + 1) * w],
+                in_=values[:, PACK * part * w : PACK * (part + 1) * w],
+            )
+
+        def transpose_x(r, half):
+            bank = banks.tile([P, BANK], F32, name="bank")
+            x_bank[(r, half)] = bank
+            words = x_sb[r][:].bitcast(F32)
+            for j in range(2):
+                for u in range(2):
+                    first = (2 * half + j) * (D // 2)
+                    place = (2 * j + u) * P
+                    nc.tensor.transpose(
+                        bank[:, place : place + P], words[:, first + u : first + 2 * P : 2], identity[:]
+                    )
+
+        def copy_x(r, half):
+            if half == 0:
+                x_values[r] = ring.tile([P, ROUND * D], BF16, name="x_values", align_bytes=64)
+            dst = x_values[r][:].bitcast(F32)[:, BANK * half : BANK * (half + 1)]
+            dst = dst.rearrange("p (j r u) -> p j r u", j=2, r=P, u=2)
+            src = x_bank[(r, half)][:].rearrange("p (j u r) -> p j r u", j=2, u=2, r=P)
+            if x_copy_engine(r) == "scalar":
+                nc.scalar.copy(out=dst, in_=src)
+            else:
+                nc.vector.tensor_copy(out=dst, in_=src)
+
+        def quantise_x(r, part):
+            if part == 0:
+                x_words[r] = ring.tile([P, ROUND * P], U32, name="x_words", align_bytes=64)
+                x_scales[r] = ring.tile([P, ROUND * P], U8, name="x_scales", align_bytes=64)
+            quantise_part(x_words[r], x_scales[r], x_values[r], part, x_quantise_parts(r))
+
+        def layer1(r, j):
+            bank = banks.tile([P, BANK], F32, name="bank")
+            h_bank[(r, j)] = bank
+            tokens = slice(j * P, (j + 1) * P)
+            for q in range(4):
+                quarter = slice(q * P, (q + 1) * P)
+                nc.tensor.matmul_mx(
+                    out=bank[:, quarter],
+                    lhsT=w1_words[:, quarter].bitcast(FP8X4),
+                    lhsT_scale=w1_scales[:, quarter],
+                    rhs=x_words[r][:, tokens].bitcast(FP8X4),
+                    rhs_scale=x_scales[r][:, tokens],
+                    start=True,
+                    stop=True,
+                )
+
+        def copy_h(r, j):
+            if j == 0:
+                h_values[r] = ring.tile([P, ROUND * F], BF16, name="h_values", align_bytes=64)
+            relu_out_of_psum(
+                h_copy_engine(r, j),
+                h_values[r][:, j * F : (j + 1) * F].rearrange("p (r t) -> p r t", t=PACK),
+                h_bank[(r, j)][:].rearrange("p (t r) -> p r t", t=PACK),
+            )
+
+        def quantise_h(r, part):
+            if part == 0:
+                h_words[r] = ring.tile([P, ROUND * P], U32, name="h_words", align_bytes=64)
+                h_scales[r] = ring.tile([P, ROUND * P], U8, name="h_scales", align_bytes=64)
+            quantise_part(h_words[r], h_scales[r], h_values[r], part, h_quantise_parts(r))
+
+        def layer2(r, half):
+            bank = banks.tile([P, BANK], F32, name="bank")
+            out_bank[(r, half)] = bank
+            for j in range(2):
+                tokens = slice((2 * half + j) * P, (2 * half + j + 1) * P)
+                nc.tensor.matmul_mx(
+                    out=bank[:, j * N : (j + 1) * N],
+                    lhsT=h_words[r][:, tokens].bitcast(FP8X4),
+                    lhsT_scale=h_scales[r][:, tokens],
+                    rhs=w2_words[:].bitcast(FP8X4),
+                    rhs_scale=w2_scales[:],
+                    start=True,
+                    stop=True,
+                )
+
+        def copy_out(r, half):
+            relu_out_of_psum(
+                out_copy_engine(r, half), out_sb[r][:, BANK * half : BANK * (half + 1)], out_bank[(r, half)][:]
+            )
+
+        def store(r, part):
+            w = ROUND * N // store_parts(r)
+            first = r * ROUND * N + part * w
+            nc.sync.dma_start(out=out_rows[:, first : first + w], in_=out_sb[r][:, part * w : (part + 1) * w])
+
+        def live(r):
+            return 0 <= r < ROUNDS
+
+        for q in range(4):
+            mask_w1_quarter(q)
+        for s in range(-AHEAD, ROUNDS + BEHIND):
+            if live(s - BEHIND):
+                for part in range(h_quantise_parts(s - BEHIND)):
+                    quantise_h(s - BEHIND, part)
+            if live(s + AHEAD - 1):
+                for half in range(2):
+                    copy_x(s + AHEAD - 1, half)
+            if s == 1 - AHEAD:
+                quantise_x(0, 0)
+                quantise_w1()
+                quantise_x(0, 1)
+            if s == 0:
+                mask_w2()
+            if live(s) and live(s + 1):
+                quantise_x(s + 1, 0)
+            if s == 0:
+                quantise_w2()
+            if live(s):
+                for j in range(ROUND):
+                    layer1(s, j)
+                for j in range(ROUND):
+                    copy_h(s, j)
+            if live(s - BEHIND):
+                for half in range(2):
+                    layer2(s - BEHIND, half)
+                for half in range(2):
+                    copy_out(s - BEHIND, half)
+                for part in range(store_parts(s - BEHIND)):
+                    store(s - BEHIND, part)
+            if live(s + AHEAD):
+                for half in range(2):
+                    transpose_x(s + AHEAD, half)

@@ -94,6 +94,14 @@ def tile_sparse_connect_t_kernel(tc, x, th1, sign1, th2, sign2, relu, out):
         nc.vector.memset(warm_in[:], 0.0)
         nc.scalar.activation(out=warm_out[:], in_=warm_in[:], func=ACT.Relu)
 
+        zeros = keep.tile([P, BANK], BF16, name="zeros")
+        nc.vector.memset(zeros[:], 0.0)
+
+        def warm_tensor(count):
+            bank = banks.tile([P, BANK], F32, name="bank")
+            for i in range(count):
+                nc.tensor.matmul(bank[:], lhsT=zeros[:, :P], rhs=zeros[:], start=True, stop=True)
+
         w1_values = keep.tile([P, PACK * F], BF16, name="w1_values", align_bytes=64)
         w1_words = keep.tile([P, F], U32, name="w1_words", align_bytes=64)
         w1_scales = keep.tile([P, F], U8, name="w1_scales", align_bytes=64)
@@ -239,6 +247,7 @@ def tile_sparse_connect_t_kernel(tc, x, th1, sign1, th2, sign2, relu, out):
         def live(r):
             return 0 <= r < ROUNDS
 
+        warm_tensor(8)
         for q in range(4):
             mask_w1_quarter(q)
         for s in range(-AHEAD, ROUNDS + BEHIND):
@@ -273,3 +282,5 @@ def tile_sparse_connect_t_kernel(tc, x, th1, sign1, th2, sign2, relu, out):
             if live(s + AHEAD):
                 for half in range(2):
                     transpose_x(s + AHEAD, half)
+                if s < 0:
+                    warm_tensor(2)

@@ -282,5 +282,5 @@ def tile_sparse_connect_t_kernel(tc, x, th1, sign1, th2, sign2, relu, out):
             if live(s + AHEAD):
                 for half in range(2):
                     transpose_x(s + AHEAD, half)
-                if s < 0:
+                if s == -AHEAD:
                     warm_tensor(2)

@@ -32,11 +32,13 @@ def x_copy_engine(r):
 
 
 def h_copy_engine(r, j):
-    return "vector" if (r, j) in ((ROUNDS - 2, 1), (ROUNDS - 2, 2), (ROUNDS - 1, 0), (ROUNDS - 1, 1)) else "scalar"
+    return "vector" if r == ROUNDS - 1 or (r, j) == (ROUNDS - 2, 2) else "scalar"
 
 
-def out_copy_engine(r, half):
-    if half == 0 or r in (4, ROUNDS - 4, ROUNDS - 3, ROUNDS - 2):
+def out_copy_engine(r, part):
+    if r == ROUNDS - 1:
+        return ("scalar", "scalar", "vector", "scalar")[part]
+    if part == 0 or r in (4, ROUNDS - 4, ROUNDS - 3, ROUNDS - 2):
         return "scalar"
     return "vector"
 
@@ -49,8 +51,12 @@ def h_quantise_parts(r):
     return 2 if r >= ROUNDS - 2 else 1
 
 
+def out_parts(r):
+    return 4 if r == ROUNDS - 1 else 2
+
+
 def store_parts(r):
-    return 2 if r >= ROUNDS - 3 else 1
+    return out_parts(r) if r >= ROUNDS - 3 else 1
 
 
 def tile_sparse_connect_t_kernel(tc, x, th1, sign1, th2, sign2, relu, out):
@@ -109,27 +115,26 @@ def tile_sparse_connect_t_kernel(tc, x, th1, sign1, th2, sign2, relu, out):
         w2_words = keep.tile([P, N], U32, name="w2_words", align_bytes=64)
         w2_scales = keep.tile([P, N], U8, name="w2_scales", align_bytes=64)
 
+        def positive(th_sb):
+            nc.vector.tensor_scalar_max(out=th_sb[:], in0=th_sb[:], scalar1=0.0)
+
         def mask_w1_quarter(q):
-            nc.vector.scalar_tensor_tensor(
-                out=w1_values[:].rearrange("p (q m t) -> p q m t", q=4, m=P, t=PACK)[:, q],
-                in0=th1_sb[:].rearrange("p (t m q) -> p q m t", t=PACK, m=P, q=4)[:, q],
-                scalar=0.0,
-                in1=sign1_sb[:].rearrange("p (t m q) -> p q m t", t=PACK, m=P, q=4)[:, q],
-                op0=ALU.max,
-                op1=ALU.mult,
+            nc.vector.tensor_tensor(
+                out=w1_values[:].rearrange("p (q c i t) -> p q c t i", q=4, c=P // 4, i=4, t=PACK)[:, q],
+                in0=th1_sb[:].rearrange("p (t c i q) -> p q c t i", t=PACK, c=P // 4, i=4, q=4)[:, q],
+                in1=sign1_sb[:].rearrange("p (t c i q) -> p q c t i", t=PACK, c=P // 4, i=4, q=4)[:, q],
+                op=ALU.mult,
             )
 
         def quantise_w1():
             nc.vector.quantize_mx(out=w1_words[:].bitcast(FP8X4), scales=w1_scales[:], in_=w1_values[:])
 
         def mask_w2():
-            nc.vector.scalar_tensor_tensor(
-                out=w2_values[:].rearrange("p (n t) -> p n t", t=PACK),
-                in0=th2_sb[:].rearrange("p (t n) -> p n t", t=PACK),
-                scalar=0.0,
-                in1=sign2_sb[:].rearrange("p (t n) -> p n t", t=PACK),
-                op0=ALU.max,
-                op1=ALU.mult,
+            nc.vector.tensor_tensor(
+                out=w2_values[:].rearrange("p (c i t) -> p c t i", i=4, t=PACK),
+                in0=th2_sb[:].rearrange("p (t c i) -> p c t i", t=PACK, i=4),
+                in1=sign2_sb[:].rearrange("p (t c i) -> p c t i", t=PACK, i=4),
+                op=ALU.mult,
             )
 
         def quantise_w2():
@@ -219,11 +224,12 @@ def tile_sparse_connect_t_kernel(tc, x, th1, sign1, th2, sign2, relu, out):
                 h_scales[r] = ring.tile([P, ROUND * P], U8, name="h_scales", align_bytes=64)
             quantise_part(h_words[r], h_scales[r], h_values[r], part, h_quantise_parts(r))
 
-        def layer2(r, half):
+        def layer2(r, part):
             bank = banks.tile([P, BANK], F32, name="bank")
-            out_bank[(r, half)] = bank
-            for j in range(2):
-                tokens = slice((2 * half + j) * P, (2 * half + j + 1) * P)
+            out_bank[(r, part)] = bank
+            tiles = ROUND // out_parts(r)
+            for j in range(tiles):
+                tokens = slice((tiles * part + j) * P, (tiles * part + j + 1) * P)
                 nc.tensor.matmul_mx(
                     out=bank[:, j * N : (j + 1) * N],
                     lhsT=h_words[r][:, tokens].bitcast(FP8X4),
@@ -234,9 +240,10 @@ def tile_sparse_connect_t_kernel(tc, x, th1, sign1, th2, sign2, relu, out):
                     stop=True,
                 )
 
-        def copy_out(r, half):
+        def copy_out(r, part):
+            w = ROUND * N // out_parts(r)
             relu_out_of_psum(
-                out_copy_engine(r, half), out_sb[r][:, BANK * half : BANK * (half + 1)], out_bank[(r, half)][:]
+                out_copy_engine(r, part), out_sb[r][:, w * part : w * (part + 1)], out_bank[(r, part)][:, :w]
             )
 
         def store(r, part):
@@ -248,12 +255,12 @@ def tile_sparse_connect_t_kernel(tc, x, th1, sign1, th2, sign2, relu, out):
             return 0 <= r < ROUNDS
 
         warm_tensor(8)
+        positive(th1_sb)
         for q in range(4):
             mask_w1_quarter(q)
         for s in range(-AHEAD, ROUNDS + BEHIND):
-            if live(s - BEHIND):
-                for part in range(h_quantise_parts(s - BEHIND)):
-                    quantise_h(s - BEHIND, part)
+            if live(s - BEHIND) and s < ROUNDS:
+                quantise_h(s - BEHIND, 0)
             if live(s + AHEAD - 1):
                 for half in range(2):
                     copy_x(s + AHEAD - 1, half)
@@ -262,6 +269,7 @@ def tile_sparse_connect_t_kernel(tc, x, th1, sign1, th2, sign2, relu, out):
                 quantise_w1()
                 quantise_x(0, 1)
             if s == 0:
+                positive(th2_sb)
                 mask_w2()
             if live(s) and live(s + 1):
                 quantise_x(s + 1, 0)
@@ -270,13 +278,17 @@ def tile_sparse_connect_t_kernel(tc, x, th1, sign1, th2, sign2, relu, out):
             if live(s):
                 for j in range(ROUND):
                     layer1(s, j)
-                for j in range(ROUND):
+                for j in range(ROUND - 1 if s == ROUNDS - 2 else ROUND):
                     copy_h(s, j)
+                    if s == ROUNDS - 1:
+                        quantise_h(s - 1 + j // 2, j % 2)
             if live(s - BEHIND):
-                for half in range(2):
-                    layer2(s - BEHIND, half)
-                for half in range(2):
-                    copy_out(s - BEHIND, half)
+                for part in range(out_parts(s - BEHIND)):
+                    layer2(s - BEHIND, part)
+                for part in range(out_parts(s - BEHIND)):
+                    copy_out(s - BEHIND, part)
+                if s == ROUNDS - 2:
+                    copy_h(s, ROUND - 1)
                 for part in range(store_parts(s - BEHIND)):
                     store(s - BEHIND, part)
             if live(s + AHEAD):

@@ -47,6 +47,10 @@ def x_quantise_parts(r):
     return 2 if r == 0 else 1
 
 
+def x_load_parts(r):
+    return 2 if r < 2 else 1
+
+
 def h_quantise_parts(r):
     return 2 if r >= ROUNDS - 2 else 1
 
@@ -78,14 +82,22 @@ def tile_sparse_connect_t_kernel(tc, x, th1, sign1, th2, sign2, relu, out):
         x_sb = [keep.tile([P, ROUND * D], BF16, name="x_sb%d" % r) for r in range(ROUNDS)]
         out_sb = [keep.tile([P, ROUND * N], F32, name="out_sb%d" % r) for r in range(ROUNDS)]
 
-        def load_w(dst, src):
-            nc.sync.dma_start(out=dst[:], in_=src.rearrange("(p t) n -> p (t n)", t=PACK))
+        def load_w(dst, src, part=0, parts=1):
+            w = dst.shape[1] // parts
+            run = slice(part * w, (part + 1) * w)
+            nc.sync.dma_start(out=dst[:, run], in_=src.rearrange("(p t) n -> p (t n)", t=PACK)[:, run])
 
         def load_x(r):
-            nc.sync.dma_start(out=x_sb[r][:], in_=x_rows[:, r * ROUND * D : (r + 1) * ROUND * D])
+            w = ROUND * D // x_load_parts(r)
+            for part in range(x_load_parts(r)):
+                first = r * ROUND * D + part * w
+                nc.sync.dma_start(
+                    out=x_sb[r][:, part * w : (part + 1) * w], in_=x_rows[:, first : first + w]
+                )
 
-        load_w(th1_sb, th1)
-        load_w(sign1_sb, sign1)
+        for part in range(2):
+            load_w(th1_sb, th1, part, 2)
+            load_w(sign1_sb, sign1, part, 2)
         for r in range(AHEAD):
             load_x(r)
         load_w(th2_sb, th2)
@@ -115,21 +127,30 @@ def tile_sparse_connect_t_kernel(tc, x, th1, sign1, th2, sign2, relu, out):
         w2_words = keep.tile([P, N], U32, name="w2_words", align_bytes=64)
         w2_scales = keep.tile([P, N], U8, name="w2_scales", align_bytes=64)
 
-        def positive(th_sb):
-            nc.vector.tensor_scalar_max(out=th_sb[:], in0=th_sb[:], scalar1=0.0)
+        def mask_w1_rows(part):
+            w = PACK * F // 2
+            run = slice(part * w, (part + 1) * w)
+            nc.vector.tensor_scalar_max(out=th1_sb[:, run], in0=th1_sb[:, run], scalar1=0.0)
+            nc.vector.tensor_tensor(out=th1_sb[:, run], in0=th1_sb[:, run], in1=sign1_sb[:, run], op=ALU.mult)
 
-        def mask_w1_quarter(q):
-            nc.vector.tensor_tensor(
-                out=w1_values[:].rearrange("p (q c i t) -> p q c t i", q=4, c=P // 4, i=4, t=PACK)[:, q],
-                in0=th1_sb[:].rearrange("p (t c i q) -> p q c t i", t=PACK, c=P // 4, i=4, q=4)[:, q],
-                in1=sign1_sb[:].rearrange("p (t c i q) -> p q c t i", t=PACK, c=P // 4, i=4, q=4)[:, q],
-                op=ALU.mult,
+        def interleave_w1_quarter(q):
+            dst = w1_values[:].rearrange("p (q c i t) -> p q c t i", q=4, c=P // 4, i=4, t=PACK)[:, q]
+            src = th1_sb[:].rearrange("p (t c i q) -> p q c t i", t=PACK, c=P // 4, i=4, q=4)[:, q]
+            if q == 3:
+                nc.scalar.copy(out=dst, in_=src)
+            else:
+                nc.vector.tensor_copy(out=dst, in_=src)
+
+        def quantise_w1(part):
+            cols = slice(part * F // 2, (part + 1) * F // 2)
+            nc.vector.quantize_mx(
+                out=w1_words[:, cols].bitcast(FP8X4),
+                scales=w1_scales[:, cols],
+                in_=w1_values[:, PACK * cols.start : PACK * cols.stop],
             )
 
-        def quantise_w1():
-            nc.vector.quantize_mx(out=w1_words[:].bitcast(FP8X4), scales=w1_scales[:], in_=w1_values[:])
-
         def mask_w2():
+            nc.vector.tensor_scalar_max(out=th2_sb[:], in0=th2_sb[:], scalar1=0.0)
             nc.vector.tensor_tensor(
                 out=w2_values[:].rearrange("p (c i t) -> p c t i", i=4, t=PACK),
                 in0=th2_sb[:].rearrange("p (t c i) -> p c t i", t=PACK, i=4),
@@ -255,9 +276,12 @@ def tile_sparse_connect_t_kernel(tc, x, th1, sign1, th2, sign2, relu, out):
             return 0 <= r < ROUNDS
 
         warm_tensor(8)
-        positive(th1_sb)
+        for part in range(2):
+            mask_w1_rows(part)
         for q in range(4):
-            mask_w1_quarter(q)
+            interleave_w1_quarter(q)
+        for part in range(2):
+            quantise_w1(part)
         for s in range(-AHEAD, ROUNDS + BEHIND):
             if live(s - BEHIND) and s < ROUNDS:
                 quantise_h(s - BEHIND, 0)
@@ -266,10 +290,8 @@ def tile_sparse_connect_t_kernel(tc, x, th1, sign1, th2, sign2, relu, out):
                     copy_x(s + AHEAD - 1, half)
             if s == 1 - AHEAD:
                 quantise_x(0, 0)
-                quantise_w1()
                 quantise_x(0, 1)
             if s == 0:
-                positive(th2_sb)
                 mask_w2()
             if live(s) and live(s + 1):
                 quantise_x(s + 1, 0)

@@ -59,6 +59,10 @@ def out_parts(r):
     return 4 if r == ROUNDS - 1 else 2
 
 
+def lagged(r):
+    return out_copy_engine(r, 1) == "vector" and store_parts(r) == 1
+
+
 def store_parts(r):
     return out_parts(r) if r >= ROUNDS - 3 else 1
 
@@ -285,6 +289,9 @@ def tile_sparse_connect_t_kernel(tc, x, th1, sign1, th2, sign2, relu, out):
         for s in range(-AHEAD, ROUNDS + BEHIND):
             if live(s - BEHIND) and s < ROUNDS:
                 quantise_h(s - BEHIND, 0)
+            if live(s - BEHIND - 1) and lagged(s - BEHIND - 1):
+                copy_out(s - BEHIND - 1, 1)
+                store(s - BEHIND - 1, 0)
             if live(s + AHEAD - 1):
                 for half in range(2):
                     copy_x(s + AHEAD - 1, half)
@@ -308,11 +315,13 @@ def tile_sparse_connect_t_kernel(tc, x, th1, sign1, th2, sign2, relu, out):
                 for part in range(out_parts(s - BEHIND)):
                     layer2(s - BEHIND, part)
                 for part in range(out_parts(s - BEHIND)):
-                    copy_out(s - BEHIND, part)
+                    if not (part == 1 and lagged(s - BEHIND)):
+                        copy_out(s - BEHIND, part)
                 if s == ROUNDS - 2:
                     copy_h(s, ROUND - 1)
-                for part in range(store_parts(s - BEHIND)):
-                    store(s - BEHIND, part)
+                if not lagged(s - BEHIND):
+                    for part in range(store_parts(s - BEHIND)):
+                        store(s - BEHIND, part)
             if live(s + AHEAD):
                 for half in range(2):
                     transpose_x(s + AHEAD, half)

from contextlib import ExitStack

import concourse.masks as masks
import concourse.mybir as mybir

F32 = mybir.dt.float32
BF16 = mybir.dt.bfloat16
U32 = mybir.dt.uint32
U8 = mybir.dt.uint8
FP8X4 = mybir.dt.float8_e4m3fn_x4
ALU = mybir.AluOpType
ACT = mybir.ActivationFunctionType

P = 128
PACK = 4
TOKENS = 8192
D = 512
F = 512
N = 256
BANK = 512
TILES = TOKENS // P
ROUND = 4
ROUNDS = TILES // ROUND
AHEAD = 3
BEHIND = 2

FLOPS = 2 * TOKENS * D * (F + N)


def x_copy_engine(r):
    return "scalar" if r < AHEAD else "vector"


def h_copy_engine(r, j):
    return "vector" if r == ROUNDS - 1 or (r, j) == (ROUNDS - 2, 2) else "scalar"


def out_copy_engine(r, part):
    if r == ROUNDS - 1:
        return ("scalar", "scalar", "vector", "scalar")[part]
    if part == 0 or r in (4, ROUNDS - 4, ROUNDS - 3, ROUNDS - 2):
        return "scalar"
    return "vector"


def x_quantise_parts(r):
    return 2 if r == 0 else 1


def x_load_parts(r):
    return 2 if r < 2 else 1


def h_quantise_parts(r):
    return 2 if r >= ROUNDS - 2 else 1


def out_parts(r):
    return 4 if r == ROUNDS - 1 else 2


def lagged(r):
    return out_copy_engine(r, 1) == "vector" and store_parts(r) == 1


def store_parts(r):
    return out_parts(r) if r >= ROUNDS - 3 else 1


def tile_sparse_connect_t_kernel(tc, x, th1, sign1, th2, sign2, relu, out):
    assert relu == 1
    nc = tc.nc
    x_rows = x.flatten_outer_dims().rearrange("(p j) k -> p (j k)", j=TILES)
    out_rows = out.flatten_outer_dims().rearrange("(p j) n -> p (j n)", j=TILES)

    with ExitStack() as ctx:
        ctx.enter_context(tc.manual_schedule())
        keep = ctx.enter_context(tc.tile_pool(name="keep", bufs=1))
        ring = ctx.enter_context(tc.tile_pool(name="ring", bufs=4))
        banks = ctx.enter_context(tc.psum_pool(name="banks", bufs=8))

        th1_sb = keep.tile([P, PACK * F], BF16, name="th1_sb")
        sign1_sb = keep.tile([P, PACK * F], BF16, name="sign1_sb")
        th2_sb = keep.tile([P, PACK * N], BF16, name="th2_sb")
        sign2_sb = keep.tile([P, PACK * N], BF16, name="sign2_sb")
        x_sb = [keep.tile([P, ROUND * D], BF16, name="x_sb%d" % r) for r in range(ROUNDS)]
        out_sb = [keep.tile([P, ROUND * N], F32, name="out_sb%d" % r) for r in range(ROUNDS)]

        def load_w(dst, src, part=0, parts=1):
            w = dst.shape[1] // parts
            run = slice(part * w, (part + 1) * w)
            nc.sync.dma_start(out=dst[:, run], in_=src.rearrange("(p t) n -> p (t n)", t=PACK)[:, run])

        def load_x(r):
            w = ROUND * D // x_load_parts(r)
            for part in range(x_load_parts(r)):
                first = r * ROUND * D + part * w
                nc.sync.dma_start(
                    out=x_sb[r][:, part * w : (part + 1) * w], in_=x_rows[:, first : first + w]
                )

        for part in range(2):
            load_w(th1_sb, th1, part, 2)
            load_w(sign1_sb, sign1, part, 2)
        for r in range(AHEAD):
            load_x(r)
        load_w(th2_sb, th2)
        load_w(sign2_sb, sign2)
        for r in range(AHEAD, ROUNDS):
            load_x(r)

        identity = keep.tile([P, P], F32, name="identity")
        masks.make_identity(nc, identity[:])
        warm_in = keep.tile([P, 1], F32, name="warm_in")
        warm_out = keep.tile([P, 1], F32, name="warm_out")
        nc.vector.memset(warm_in[:], 0.0)
        nc.scalar.activation(out=warm_out[:], in_=warm_in[:], func=ACT.Relu)

        zeros = keep.tile([P, BANK], BF16, name="zeros")
        nc.vector.memset(zeros[:], 0.0)

        def warm_tensor(count):
            bank = banks.tile([P, BANK], F32, name="bank")
            for i in range(count):
                nc.tensor.matmul(bank[:], lhsT=zeros[:, :P], rhs=zeros[:], start=True, stop=True)

        w1_values = keep.tile([P, PACK * F], BF16, name="w1_values", align_bytes=64)
        w1_words = keep.tile([P, F], U32, name="w1_words", align_bytes=64)
        w1_scales = keep.tile([P, F], U8, name="w1_scales", align_bytes=64)
        w2_values = keep.tile([P, PACK * N], BF16, name="w2_values", align_bytes=64)
        w2_words = keep.tile([P, N], U32, name="w2_words", align_bytes=64)
        w2_scales = keep.tile([P, N], U8, name="w2_scales", align_bytes=64)

        def mask_w1_rows(part):
            w = PACK * F // 2
            run = slice(part * w, (part + 1) * w)
            nc.vector.tensor_scalar_max(out=th1_sb[:, run], in0=th1_sb[:, run], scalar1=0.0)
            nc.vector.tensor_tensor(out=th1_sb[:, run], in0=th1_sb[:, run], in1=sign1_sb[:, run], op=ALU.mult)

        def interleave_w1_quarter(q):
            dst = w1_values[:].rearrange("p (q c i t) -> p q c t i", q=4, c=P // 4, i=4, t=PACK)[:, q]
            src = th1_sb[:].rearrange("p (t c i q) -> p q c t i", t=PACK, c=P // 4, i=4, q=4)[:, q]
            if q == 3:
                nc.scalar.copy(out=dst, in_=src)
            else:
                nc.vector.tensor_copy(out=dst, in_=src)

        def quantise_w1(part):
            cols = slice(part * F // 2, (part + 1) * F // 2)
            nc.vector.quantize_mx(
                out=w1_words[:, cols].bitcast(FP8X4),
                scales=w1_scales[:, cols],
                in_=w1_values[:, PACK * cols.start : PACK * cols.stop],
            )

        def mask_w2():
            nc.vector.tensor_scalar_max(out=th2_sb[:], in0=th2_sb[:], scalar1=0.0)
            nc.vector.tensor_tensor(
                out=w2_values[:].rearrange("p (c i t) -> p c t i", i=4, t=PACK),
                in0=th2_sb[:].rearrange("p (t c i) -> p c t i", t=PACK, i=4),
                in1=sign2_sb[:].rearrange("p (t c i) -> p c t i", t=PACK, i=4),
                op=ALU.mult,
            )

        def quantise_w2():
            nc.vector.quantize_mx(out=w2_words[:].bitcast(FP8X4), scales=w2_scales[:], in_=w2_values[:])

        x_bank = {}
        x_values = {}
        x_words = {}
        x_scales = {}
        h_bank = {}
        h_values = {}
        h_words = {}
        h_scales = {}
        out_bank = {}

        def relu_out_of_psum(engine, dst, src):
            if engine == "scalar":
                nc.scalar.activation(out=dst, in_=src, func=ACT.Relu)
            else:
                nc.vector.tensor_scalar_max(out=dst, in0=src, scalar1=0.0)

        def quantise_part(words, scales, values, part, parts):
            w = ROUND * P // parts
            nc.vector.quantize_mx(
                out=words[:, part * w : (part + 1) * w].bitcast(FP8X4),
                scales=scales[:, part * w : (part + 1) * w],
                in_=values[:, PACK * part * w : PACK * (part + 1) * w],
            )

        def transpose_x(r, half):
            bank = banks.tile([P, BANK], F32, name="bank")
            x_bank[(r, half)] = bank
            words = x_sb[r][:].bitcast(F32)
            for j in range(2):
                for u in range(2):
                    first = (2 * half + j) * (D // 2)
                    place = (2 * j + u) * P
                    nc.tensor.transpose(
                        bank[:, place : place + P], words[:, first + u : first + 2 * P : 2], identity[:]
                    )

        def copy_x(r, half):
            if half == 0:
                x_values[r] = ring.tile([P, ROUND * D], BF16, name="x_values", align_bytes=64)
            dst = x_values[r][:].bitcast(F32)[:, BANK * half : BANK * (half + 1)]
            dst = dst.rearrange("p (j r u) -> p j r u", j=2, r=P, u=2)
            src = x_bank[(r, half)][:].rearrange("p (j u r) -> p j r u", j=2, u=2, r=P)
            if x_copy_engine(r) == "scalar":
                nc.scalar.copy(out=dst, in_=src)
            else:
                nc.vector.tensor_copy(out=dst, in_=src)

        def quantise_x(r, part):
            if part == 0:
                x_words[r] = ring.tile([P, ROUND * P], U32, name="x_words", align_bytes=64)
                x_scales[r] = ring.tile([P, ROUND * P], U8, name="x_scales", align_bytes=64)
            quantise_part(x_words[r], x_scales[r], x_values[r], part, x_quantise_parts(r))

        def layer1(r, j):
            bank = banks.tile([P, BANK], F32, name="bank")
            h_bank[(r, j)] = bank
            tokens = slice(j * P, (j + 1) * P)
            for q in range(4):
                quarter = slice(q * P, (q + 1) * P)
                nc.tensor.matmul_mx(
                    out=bank[:, quarter],
                    lhsT=w1_words[:, quarter].bitcast(FP8X4),
                    lhsT_scale=w1_scales[:, quarter],
                    rhs=x_words[r][:, tokens].bitcast(FP8X4),
                    rhs_scale=x_scales[r][:, tokens],
                    start=True,
                    stop=True,
                )

        def copy_h(r, j):
            if j == 0:
                h_values[r] = ring.tile([P, ROUND * F], BF16, name="h_values", align_bytes=64)
            relu_out_of_psum(
                h_copy_engine(r, j),
                h_values[r][:, j * F : (j + 1) * F].rearrange("p (r t) -> p r t", t=PACK),
                h_bank[(r, j)][:].rearrange("p (t r) -> p r t", t=PACK),
            )

        def quantise_h(r, part):
            if part == 0:
                h_words[r] = ring.tile([P, ROUND * P], U32, name="h_words", align_bytes=64)
                h_scales[r] = ring.tile([P, ROUND * P], U8, name="h_scales", align_bytes=64)
            quantise_part(h_words[r], h_scales[r], h_values[r], part, h_quantise_parts(r))

        def layer2(r, part):
            bank = banks.tile([P, BANK], F32, name="bank")
            out_bank[(r, part)] = bank
            tiles = ROUND // out_parts(r)
            for j in range(tiles):
                tokens = slice((tiles * part + j) * P, (tiles * part + j + 1) * P)
                nc.tensor.matmul_mx(
                    out=bank[:, j * N : (j + 1) * N],
                    lhsT=h_words[r][:, tokens].bitcast(FP8X4),
                    lhsT_scale=h_scales[r][:, tokens],
                    rhs=w2_words[:].bitcast(FP8X4),
                    rhs_scale=w2_scales[:],
                    start=True,
                    stop=True,
                )

        def copy_out(r, part):
            w = ROUND * N // out_parts(r)
            relu_out_of_psum(
                out_copy_engine(r, part), out_sb[r][:, w * part : w * (part + 1)], out_bank[(r, part)][:, :w]
            )

        def store(r, part):
            w = ROUND * N // store_parts(r)
            first = r * ROUND * N + part * w
            nc.sync.dma_start(out=out_rows[:, first : first + w], in_=out_sb[r][:, part * w : (part + 1) * w])

        def live(r):
            return 0 <= r < ROUNDS

        warm_tensor(8)
        for part in range(2):
            mask_w1_rows(part)
        for q in range(4):
            interleave_w1_quarter(q)
        for part in range(2):
            quantise_w1(part)
        for s in range(-AHEAD, ROUNDS + BEHIND):
            if live(s - BEHIND) and s < ROUNDS:
                quantise_h(s - BEHIND, 0)
            if live(s - BEHIND - 1) and lagged(s - BEHIND - 1):
                copy_out(s - BEHIND - 1, 1)
                store(s - BEHIND - 1, 0)
            if live(s + AHEAD - 1):
                for half in range(2):
                    copy_x(s + AHEAD - 1, half)
            if s == 1 - AHEAD:
                quantise_x(0, 0)
                quantise_x(0, 1)
            if s == 0:
                mask_w2()
            if live(s) and live(s + 1):
                quantise_x(s + 1, 0)
            if s == 0:
                quantise_w2()
            if live(s):
                for j in range(ROUND):
                    layer1(s, j)
                for j in range(ROUND - 1 if s == ROUNDS - 2 else ROUND):
                    copy_h(s, j)
                    if s == ROUNDS - 1:
                        quantise_h(s - 1 + j // 2, j % 2)
            if live(s - BEHIND):
                for part in range(out_parts(s - BEHIND)):
                    layer2(s - BEHIND, part)
                for part in range(out_parts(s - BEHIND)):
                    if not (part == 1 and lagged(s - BEHIND)):
                        copy_out(s - BEHIND, part)
                if s == ROUNDS - 2:
                    copy_h(s, ROUND - 1)
                if not lagged(s - BEHIND):
                    for part in range(store_parts(s - BEHIND)):
                        store(s - BEHIND, part)
            if live(s + AHEAD):
                for half in range(2):
                    transpose_x(s + AHEAD, half)
                if s == -AHEAD:
                    warm_tensor(2)
